import numpy as np
import ml_dtypes


def mxq(x, axis, fmt="e4m3"):
    dtype, down = {"e4m3": (ml_dtypes.float8_e4m3fn, 7), "e5m2": (ml_dtypes.float8_e5m2, 14)}[fmt]
    v = np.moveaxis(np.asarray(x, np.float32).astype(ml_dtypes.bfloat16).astype(np.float64), axis, -1)
    blocks = v.reshape(v.shape[:-1] + (-1, 32))
    amax = np.abs(blocks).max(-1, keepdims=True)
    byte = np.maximum(np.where(amax > 0, np.frexp(amax)[1] - 1 + 127, 0) - down, 1)
    scale = np.exp2(byte - 127.0)
    codes = (blocks / scale).astype(np.float32).astype(dtype).astype(np.float64)
    return np.moveaxis((codes * scale).reshape(v.shape), -1, axis)


WIDE = False


def mx_kscale(k):
    if not WIDE:
        return np.ones(k)
    levels = np.array([10, -10, 5, -5, 0])
    a = np.random.permutation(np.resize(levels, k // 512 * 4)).reshape(k // 512, 4)
    idx = np.arange(k)
    return np.exp2(a[idx // 512, idx % 128 // 32])


BF16 = ml_dtypes.bfloat16


def bf(x):
    return np.asarray(x, np.float32).astype(BF16)


def f64(x):
    return np.asarray(x).astype(np.float64)


B, T, D, N, O = 4, 2048, 512, 512, 256


def erf(x):
    a = np.minimum(np.abs(x), 5.0)
    z = 2.0 * a * a
    term = a.copy()
    tot = a.copy()
    for n in range(1, 80):
        term = term * z / (2 * n + 1)
        tot = tot + term
    return np.sign(x) * (2.0 / np.sqrt(np.pi)) * np.exp(-a * a) * tot


def gelu_erf(x):
    return 0.5 * x * (1.0 + erf(x / np.sqrt(2.0)))


def setup_inputs():
    s = mx_kscale(D)
    return {"q": bf(np.random.standard_normal((B, T, D)) * s),
            "k": bf(np.random.standard_normal((N, D)) / np.sqrt(D) / s),
            "v": bf(np.random.standard_normal((N, O)) * 1.5 / np.sqrt(N))}


def reference(q, k, v):
    scores = mxq(f64(q), 2, "e4m3") @ mxq(f64(k), 1, "e4m3").T
    sqrt_n = np.sqrt(float(scores.shape[-1]))
    norm = np.linalg.norm(scores, axis=-1, keepdims=True)
    gated = gelu_erf(scores / norm * sqrt_n)
    return mxq(gated, 2, "e4m3") @ mxq(f64(v), 0, "e4m3")

@@ -1,0 +1,241 @@
+from contextlib import ExitStack
+import math
+
+import concourse.mybir as mybir
+from concourse.masks import make_identity
+
+F32 = mybir.dt.float32
+BF16 = mybir.dt.bfloat16
+U32 = mybir.dt.uint32
+U8 = mybir.dt.uint8
+FP8X4 = mybir.dt.float8_e4m3fn_x4
+ACT = mybir.ActivationFunctionType
+ALU = mybir.AluOpType
+
+P = 128
+TOKENS = 8192
+D = 512
+NB = 512
+O = 256
+FLOPS = 2 * TOKENS * D * NB + 2 * TOKENS * NB * O
+CHUNKS = (2, 2, 4, 8, 8, 8, 8, 8, 8, 8)
+NP = TOKENS // (2 * P)
+
+
+def tile_pinard_t_kernel(tc, q, k, v, out):
+    nc = tc.nc
+    qf = q.flatten_outer_dims()
+    of = out.flatten_outer_dims()
+    with ExitStack() as ctx:
+        const = ctx.enter_context(tc.tile_pool(name="const", bufs=1))
+        qpool = ctx.enter_context(tc.tile_pool(name="qpool", bufs=1))
+        work = ctx.enter_context(tc.tile_pool(name="work", bufs=2))
+        psum = ctx.enter_context(tc.psum_pool(name="psum", bufs=1))
+        ctx.enter_context(tc.manual_schedule())
+
+        k_sb = const.tile([P, 4, D], BF16, name="k_sb")
+        nc.sync.dma_start(out=k_sb[:], in_=k.rearrange("(p t) d -> p t d", t=4))
+        v_sb = const.tile([P, 4, O], BF16, name="v_sb")
+        src = []
+        row = 0
+        for c, rows in enumerate(CHUNKS):
+            qt = qpool.tile([P, rows, D], BF16, name="q%d" % c, tag="q%d" % c)
+            nc.sync.dma_start(
+                out=qt[:], in_=qf[row : row + P * rows, :].rearrange("(p r) d -> p r d", r=rows)
+            )
+            ov = of[row : row + P * rows, :].rearrange("(p r) o -> p r o", r=rows)
+            for r0 in range(0, rows, 2):
+                src.append((qt, r0, ov))
+            row += P * rows
+            if c == 1:
+                nc.sync.dma_start(out=v_sb[:], in_=v.rearrange("(p j) o -> p j o", j=4))
+
+        warm = const.tile([P, 1], F32, name="warm")
+        warm2 = const.tile([P, 1], F32, name="warm2")
+        neghalf = const.tile([P, 1], F32, name="neghalf")
+        nc.vector.memset(warm[:], 0.0)
+        nc.vector.memset(neghalf[:], -0.5)
+        nc.scalar.activation(out=warm2[:], in_=warm[:], func=ACT.Gelu)
+        ident_f = const.tile([P, P], F32, name="ident_f")
+        make_identity(nc, ident_f[:])
+        ident_b = const.tile([P, P], BF16, name="ident_b")
+        make_identity(nc, ident_b[:])
+        junk = const.tile([P, NB], BF16, name="junk")
+
+        def flip_pair(dst, rows):
+            for i in range(2):
+                words = rows[i].bitcast(F32)
+                for u in range(2):
+                    nc.tensor.transpose(dst[:, i, u, :], words[:, u * P : (u + 1) * P], ident_f[:])
+
+        def regroup_words(copy, dst, ps):
+            copy(
+                out=dst[:].bitcast(F32).rearrange("p (i t u) -> p i t u", i=2, u=2),
+                in_=ps[:].rearrange("p i u t -> p i t u"),
+            )
+
+        kw = const.tile([P, NB], U32, name="kw", align_bytes=64)
+        ks = const.tile([P, NB], U8, name="ks", align_bytes=64)
+        kgs = []
+        for h in range(2):
+            kps = psum.tile([P, 2, 2, P], F32, name="kps", tag="sc", bufs=4)
+            flip_pair(kps, [k_sb[:, 2 * h, :], k_sb[:, 2 * h + 1, :]])
+            kg = const.tile([P, 8 * P], BF16, name="kg%d" % h, align_bytes=64)
+            regroup_words(nc.vector.tensor_copy if h == 0 else nc.scalar.copy, kg, kps)
+            kgs.append(kg)
+        for h in range(2):
+            nc.vector.quantize_mx(
+                out=kw[:, 256 * h : 256 * h + 256].bitcast(FP8X4),
+                scales=ks[:, 256 * h : 256 * h + 256],
+                in_=kgs[h][:],
+            )
+        vw = const.tile([P, O], U32, name="vw", align_bytes=64)
+        vs = const.tile([P, O], U8, name="vs", align_bytes=64)
+
+        st = {}
+
+        def tq(j):
+            qt, r0, ov = src[j]
+            ps = psum.tile([P, 2, 2, P], F32, name="qT", tag="qT", bufs=1)
+            flip_pair(ps, [qt[:, r0, :], qt[:, r0 + 1, :]])
+            st[("qT", j)] = ps
+
+        def eq(j):
+            qg = work.tile([P, 8 * P], BF16, name="qg", tag="qg", bufs=2, align_bytes=64)
+            regroup_words(nc.vector.tensor_copy, qg, st[("qT", j)])
+            st[("qg", j)] = qg
+
+        def qq(j):
+            qw = work.tile([P, 2 * P], U32, name="qw", tag="qw", bufs=4, align_bytes=64)
+            qs = work.tile([P, 2 * P], U8, name="qs", tag="qs", bufs=4, align_bytes=64)
+            nc.vector.quantize_mx(out=qw[:].bitcast(FP8X4), scales=qs[:], in_=st[("qg", j)][:])
+            st[("qw", j)] = (qw, qs)
+
+        def m1(j):
+            qw, qs = st[("qw", j)]
+            for i in range(2):
+                sc = psum.tile([P, NB], F32, name="sc", tag="sc", bufs=4)
+                nc.tensor.matmul_mx(
+                    out=sc[:],
+                    lhsT=qw[:, i * P : (i + 1) * P].bitcast(FP8X4),
+                    lhsT_scale=qs[:, i * P : (i + 1) * P],
+                    rhs=kw[:].bitcast(FP8X4),
+                    rhs_scale=ks[:],
+                    start=True,
+                    stop=True,
+                )
+                st[("sc", j, i)] = sc
+
+        def sq(j, i):
+            if i == 0:
+                st[("ms", j)] = work.tile([P, 2], F32, name="ms", tag="ms", bufs=4)
+                st[("rn", j)] = work.tile([P, 2], F32, name="rn", tag="rn", bufs=4)
+            ms = st[("ms", j)]
+            rn = st[("rn", j)]
+            nc.scalar.activation(
+                out=junk[:],
+                in_=st[("sc", j, i)][:],
+                func=ACT.Square,
+                scale=1.0 / math.sqrt(float(NB)),
+                accum_out=ms[:, i : i + 1],
+            )
+            nc.gpsimd.tensor_tensor(
+                out=rn[:, i : i + 1], in0=ms[:, i : i + 1], in1=neghalf[:], op=ALU.pow
+            )
+
+        def ge(j, i):
+            if i == 0:
+                st[("g", j)] = work.tile([P, 2, NB], BF16, name="g", tag="g", bufs=2)
+            nc.scalar.activation(
+                out=st[("g", j)][:, i, :],
+                in_=st[("sc", j, i)][:],
+                func=ACT.Gelu,
+                scale=st[("rn", j)][:, i : i + 1],
+            )
+
+        def tg(j):
+            g = st[("g", j)]
+            ps = psum.tile([P, 2, 4, P], BF16, name="gT", tag="gT", bufs=1)
+            for i in range(2):
+                for t in range(4):
+                    nc.tensor.transpose(ps[:, i, t, :], g[:, i, t * P : (t + 1) * P], ident_b[:])
+            st[("gT", j)] = ps
+
+        def eg(j):
+            gg = work.tile([P, 2, P, 4], BF16, name="gg", tag="gg", bufs=2, align_bytes=64)
+            nc.vector.tensor_copy(out=gg[:], in_=st[("gT", j)][:].rearrange("p i t r -> p i r t"))
+            st[("gg", j)] = gg
+
+        def qg_(j):
+            gw = work.tile([P, 2 * P], U32, name="gw", tag="gw", bufs=4, align_bytes=64)
+            gs = work.tile([P, 2 * P], U8, name="gs", tag="gs", bufs=4, align_bytes=64)
+            nc.vector.quantize_mx(
+                out=gw[:].bitcast(FP8X4),
+                scales=gs[:],
+                in_=st[("gg", j)][:].rearrange("p i r t -> p (i r t)"),
+            )
+            st[("gw", j)] = (gw, gs)
+
+        def m2(j):
+            gw, gs = st[("gw", j)]
+            for i in range(2):
+                o_ps = psum.tile([P, O], F32, name="o%d" % i, tag="o%d" % i, bufs=1)
+                nc.tensor.matmul_mx(
+                    out=o_ps[:],
+                    lhsT=gw[:, i * P : (i + 1) * P].bitcast(FP8X4),
+                    lhsT_scale=gs[:, i * P : (i + 1) * P],
+                    rhs=vw[:].bitcast(FP8X4),
+                    rhs_scale=vs[:],
+                    start=True,
+                    stop=True,
+                )
+                st[("o", j, i)] = o_ps
+
+        def eo(j):
+            qt, r0, ov = src[j]
+            o_sb = work.tile([P, 2, O], F32, name="o_sb", tag="o_sb", bufs=4)
+            nc.scalar.copy(out=o_sb[:, 0, :], in_=st[("o", j, 0)][:])
+            nc.vector.tensor_copy(out=o_sb[:, 1, :], in_=st[("o", j, 1)][:])
+            nc.sync.dma_start(out=ov[:, r0 : r0 + 2, :], in_=o_sb[:])
+
+        def prep_v():
+            vg = const.tile([P, O, 4], BF16, name="vg", align_bytes=64)
+            nc.vector.tensor_copy(out=vg[:], in_=v_sb[:].rearrange("p j o -> p o j"))
+            return vg
+
+        def ok(j):
+            return 0 <= j < NP
+
+        vg = None
+        for kk in range(-4, NP + 3):
+            if ok(kk):
+                sq(kk, 0)
+            if ok(kk - 1):
+                ge(kk - 1, 0)
+                ge(kk - 1, 1)
+            if ok(kk + 1):
+                m1(kk + 1)
+            if ok(kk - 3):
+                m2(kk - 3)
+            if ok(kk):
+                sq(kk, 1)
+            if ok(kk - 3):
+                eo(kk - 3)
+            if ok(kk - 1):
+                tg(kk - 1)
+            if ok(kk + 4):
+                tq(kk + 4)
+            if ok(kk - 1):
+                eg(kk - 1)
+            if kk == 0:
+                vg = prep_v()
+            if ok(kk + 3):
+                qq(kk + 3)
+            if ok(kk + 4):
+                eq(kk + 4)
+            if kk == 0:
+                nc.vector.quantize_mx(
+                    out=vw[:].bitcast(FP8X4), scales=vs[:], in_=vg[:].rearrange("p o j -> p (o j)")
+                )
+            if ok(kk - 1):
+                qg_(kk - 1)

@@ -111,20 +111,19 @@ def tile_pinard_t_kernel(tc, q, k, v, out):
             nc.vector.quantize_mx(out=qw[:].bitcast(FP8X4), scales=qs[:], in_=st[("qg", j)][:])
             st[("qw", j)] = (qw, qs)
 
-        def m1(j):
+        def m1(j, i):
             qw, qs = st[("qw", j)]
-            for i in range(2):
-                sc = psum.tile([P, NB], F32, name="sc", tag="sc", bufs=4)
-                nc.tensor.matmul_mx(
-                    out=sc[:],
-                    lhsT=qw[:, i * P : (i + 1) * P].bitcast(FP8X4),
-                    lhsT_scale=qs[:, i * P : (i + 1) * P],
-                    rhs=kw[:].bitcast(FP8X4),
-                    rhs_scale=ks[:],
-                    start=True,
-                    stop=True,
-                )
-                st[("sc", j, i)] = sc
+            sc = psum.tile([P, NB], F32, name="sc", tag="sc", bufs=4)
+            nc.tensor.matmul_mx(
+                out=sc[:],
+                lhsT=qw[:, i * P : (i + 1) * P].bitcast(FP8X4),
+                lhsT_scale=qs[:, i * P : (i + 1) * P],
+                rhs=kw[:].bitcast(FP8X4),
+                rhs_scale=ks[:],
+                start=True,
+                stop=True,
+            )
+            st[("sc", j, i)] = sc
 
         def sq(j, i):
             if i == 0:
@@ -191,10 +190,14 @@ def tile_pinard_t_kernel(tc, q, k, v, out):
                 )
                 st[("o", j, i)] = o_ps
 
-        def eo(j):
-            qt, r0, ov = src[j]
+        def eo_s(j):
             o_sb = work.tile([P, 2, O], F32, name="o_sb", tag="o_sb", bufs=4)
             nc.scalar.copy(out=o_sb[:, 0, :], in_=st[("o", j, 0)][:])
+            st[("o_sb", j)] = o_sb
+
+        def eo_v(j):
+            qt, r0, ov = src[j]
+            o_sb = st[("o_sb", j)]
             nc.vector.tensor_copy(out=o_sb[:, 1, :], in_=st[("o", j, 1)][:])
             nc.sync.dma_start(out=ov[:, r0 : r0 + 2, :], in_=o_sb[:])
 
@@ -207,35 +210,40 @@ def tile_pinard_t_kernel(tc, q, k, v, out):
             return 0 <= j < NP
 
         vg = None
-        for kk in range(-4, NP + 3):
+        for kk in range(-2, NP + 3):
             if ok(kk):
                 sq(kk, 0)
-            if ok(kk - 1):
-                ge(kk - 1, 0)
-                ge(kk - 1, 1)
-            if ok(kk + 1):
-                m1(kk + 1)
+            if ok(kk - 2):
+                tg(kk - 2)
+            if ok(kk + 2):
+                tq(kk + 2)
+            if ok(kk):
+                m1(kk, 1)
             if ok(kk - 3):
                 m2(kk - 3)
+            if ok(kk - 1):
+                ge(kk - 1, 0)
+            if ok(kk + 1):
+                m1(kk + 1, 0)
+            if ok(kk - 1):
+                ge(kk - 1, 1)
             if ok(kk):
                 sq(kk, 1)
             if ok(kk - 3):
-                eo(kk - 3)
-            if ok(kk - 1):
-                tg(kk - 1)
-            if ok(kk + 4):
-                tq(kk + 4)
-            if ok(kk - 1):
-                eg(kk - 1)
+                eo_s(kk - 3)
+            if ok(kk - 2):
+                eg(kk - 2)
+            if ok(kk + 2):
+                eq(kk + 2)
             if kk == 0:
                 vg = prep_v()
-            if ok(kk + 3):
-                qq(kk + 3)
-            if ok(kk + 4):
-                eq(kk + 4)
+            if ok(kk - 2):
+                qg_(kk - 2)
+            if ok(kk + 2):
+                qq(kk + 2)
             if kk == 0:
                 nc.vector.quantize_mx(
                     out=vw[:].bitcast(FP8X4), scales=vs[:], in_=vg[:].rearrange("p o j -> p (o j)")
                 )
-            if ok(kk - 1):
-                qg_(kk - 1)
+            if ok(kk - 3):
+                eo_v(kk - 3)

@@ -33,8 +33,12 @@ def tile_pinard_t_kernel(tc, q, k, v, out):
         psum = ctx.enter_context(tc.psum_pool(name="psum", bufs=1))
         ctx.enter_context(tc.manual_schedule())
 
-        k_sb = const.tile([P, 4, D], BF16, name="k_sb")
-        nc.sync.dma_start(out=k_sb[:], in_=k.rearrange("(p t) d -> p t d", t=4))
+        kv = k.rearrange("(p t) d -> p t d", t=4)
+        k_sb = []
+        for h in range(2):
+            kt = const.tile([P, 2, D], BF16, name="k_sb%d" % h)
+            nc.sync.dma_start(out=kt[:], in_=kv[:, 2 * h : 2 * h + 2, :])
+            k_sb.append(kt)
         v_sb = const.tile([P, 4, O], BF16, name="v_sb")
         src = []
         row = 0
@@ -47,7 +51,7 @@ def tile_pinard_t_kernel(tc, q, k, v, out):
             for r0 in range(0, rows, 2):
                 src.append((qt, r0, ov))
             row += P * rows
-            if c == 1:
+            if c == 2:
                 nc.sync.dma_start(out=v_sb[:], in_=v.rearrange("(p j) o -> p j o", j=4))
 
         warm = const.tile([P, 1], F32, name="warm")
@@ -61,6 +65,19 @@ def tile_pinard_t_kernel(tc, q, k, v, out):
         ident_b = const.tile([P, P], BF16, name="ident_b")
         make_identity(nc, ident_b[:])
         junk = const.tile([P, NB], BF16, name="junk")
+        kw = const.tile([P, NB], U32, name="kw", align_bytes=64)
+        ks = const.tile([P, NB], U8, name="ks", align_bytes=64)
+        vw = const.tile([P, O], U32, name="vw", align_bytes=64)
+        vs = const.tile([P, O], U8, name="vs", align_bytes=64)
+        vg = const.tile([P, O, 4], BF16, name="vg", align_bytes=64)
+        bank_bufs = {"sc": 4, "qT": 1, "gT": 1, "o0": 1, "o1": 1}
+        st = {}
+
+        def bank(shape, dtype, tag):
+            return psum.tile(shape, dtype, name=tag, tag=tag, bufs=bank_bufs[tag])
+
+        def copy_on(scalar):
+            return nc.scalar.copy if scalar else nc.vector.tensor_copy
 
         def flip_pair(dst, rows):
             for i in range(2):
@@ -68,41 +85,35 @@ def tile_pinard_t_kernel(tc, q, k, v, out):
                 for u in range(2):
                     nc.tensor.transpose(dst[:, i, u, :], words[:, u * P : (u + 1) * P], ident_f[:])
 
-        def regroup_words(copy, dst, ps):
-            copy(
+        def regroup_words(scalar, dst, ps):
+            copy_on(scalar)(
                 out=dst[:].bitcast(F32).rearrange("p (i t u) -> p i t u", i=2, u=2),
                 in_=ps[:].rearrange("p i u t -> p i t u"),
             )
 
-        kw = const.tile([P, NB], U32, name="kw", align_bytes=64)
-        ks = const.tile([P, NB], U8, name="ks", align_bytes=64)
-        kgs = []
-        for h in range(2):
-            kps = psum.tile([P, 2, 2, P], F32, name="kps", tag="sc", bufs=4)
-            flip_pair(kps, [k_sb[:, 2 * h, :], k_sb[:, 2 * h + 1, :]])
+        def k_flip(h, scalar):
+            ps = bank([P, 2, 2, P], F32, "sc")
+            flip_pair(ps, [k_sb[h][:, 0, :], k_sb[h][:, 1, :]])
             kg = const.tile([P, 8 * P], BF16, name="kg%d" % h, align_bytes=64)
-            regroup_words(nc.vector.tensor_copy if h == 0 else nc.scalar.copy, kg, kps)
-            kgs.append(kg)
-        for h in range(2):
+            regroup_words(scalar, kg, ps)
+            st[("kg", h)] = kg
+
+        def k_quant(h):
             nc.vector.quantize_mx(
                 out=kw[:, 256 * h : 256 * h + 256].bitcast(FP8X4),
                 scales=ks[:, 256 * h : 256 * h + 256],
-                in_=kgs[h][:],
+                in_=st[("kg", h)][:],
             )
-        vw = const.tile([P, O], U32, name="vw", align_bytes=64)
-        vs = const.tile([P, O], U8, name="vs", align_bytes=64)
 
-        st = {}
-
-        def tq(j):
+        def tq(j, tag="qT"):
             qt, r0, ov = src[j]
-            ps = psum.tile([P, 2, 2, P], F32, name="qT", tag="qT", bufs=1)
+            ps = bank([P, 2, 2, P], F32, tag)
             flip_pair(ps, [qt[:, r0, :], qt[:, r0 + 1, :]])
             st[("qT", j)] = ps
 
         def eq(j):
             qg = work.tile([P, 8 * P], BF16, name="qg", tag="qg", bufs=2, align_bytes=64)
-            regroup_words(nc.vector.tensor_copy, qg, st[("qT", j)])
+            regroup_words(False, qg, st[("qT", j)])
             st[("qg", j)] = qg
 
         def qq(j):
@@ -113,7 +124,7 @@ def tile_pinard_t_kernel(tc, q, k, v, out):
 
         def m1(j, i):
             qw, qs = st[("qw", j)]
-            sc = psum.tile([P, NB], F32, name="sc", tag="sc", bufs=4)
+            sc = bank([P, NB], F32, "sc")
             nc.tensor.matmul_mx(
                 out=sc[:],
                 lhsT=qw[:, i * P : (i + 1) * P].bitcast(FP8X4),
@@ -152,72 +163,111 @@ def tile_pinard_t_kernel(tc, q, k, v, out):
                 scale=st[("rn", j)][:, i : i + 1],
             )
 
-        def tg(j):
+        def tg_tile(j, i, dst):
             g = st[("g", j)]
-            ps = psum.tile([P, 2, 4, P], BF16, name="gT", tag="gT", bufs=1)
+            for t in range(4):
+                nc.tensor.transpose(dst[:, t, :], g[:, i, t * P : (t + 1) * P], ident_b[:])
+
+        def tg(j):
+            ps = bank([P, 2, 4, P], BF16, "gT")
             for i in range(2):
-                for t in range(4):
-                    nc.tensor.transpose(ps[:, i, t, :], g[:, i, t * P : (t + 1) * P], ident_b[:])
+                tg_tile(j, i, ps[:, i, :, :])
             st[("gT", j)] = ps
 
-        def eg(j):
-            gg = work.tile([P, 2, P, 4], BF16, name="gg", tag="gg", bufs=2, align_bytes=64)
-            nc.vector.tensor_copy(out=gg[:], in_=st[("gT", j)][:].rearrange("p i t r -> p i r t"))
-            st[("gg", j)] = gg
+        def tgt(j, i, tag):
+            ps = bank([P, 4, P], BF16, tag)
+            tg_tile(j, i, ps)
+            st[("gT", j, i)] = ps
 
-        def qg_(j):
+        def new_gg(j):
+            st[("gg", j)] = work.tile([P, 2, P, 4], BF16, name="gg", tag="gg", bufs=2, align_bytes=64)
+
+        def eg(j):
+            new_gg(j)
+            nc.vector.tensor_copy(
+                out=st[("gg", j)][:], in_=st[("gT", j)][:].rearrange("p i t r -> p i r t")
+            )
+
+        def egt(j, i, scalar):
+            copy_on(scalar)(
+                out=st[("gg", j)][:, i, :, :], in_=st[("gT", j, i)][:].rearrange("p t r -> p r t")
+            )
+
+        def new_gw(j):
             gw = work.tile([P, 2 * P], U32, name="gw", tag="gw", bufs=4, align_bytes=64)
             gs = work.tile([P, 2 * P], U8, name="gs", tag="gs", bufs=4, align_bytes=64)
+            st[("gw", j)] = (gw, gs)
+
+        def qg_(j):
+            new_gw(j)
+            gw, gs = st[("gw", j)]
             nc.vector.quantize_mx(
                 out=gw[:].bitcast(FP8X4),
                 scales=gs[:],
                 in_=st[("gg", j)][:].rearrange("p i r t -> p (i r t)"),
             )
-            st[("gw", j)] = (gw, gs)
+
+        def qgt(j, i):
+            gw, gs = st[("gw", j)]
+            nc.vector.quantize_mx(
+                out=gw[:, i * P : (i + 1) * P].bitcast(FP8X4),
+                scales=gs[:, i * P : (i + 1) * P],
+                in_=st[("gg", j)][:, i, :, :].rearrange("p r t -> p (r t)"),
+            )
+
+        def m2t(j, i):
+            gw, gs = st[("gw", j)]
+            o_ps = bank([P, O], F32, "o%d" % i)
+            nc.tensor.matmul_mx(
+                out=o_ps[:],
+                lhsT=gw[:, i * P : (i + 1) * P].bitcast(FP8X4),
+                lhsT_scale=gs[:, i * P : (i + 1) * P],
+                rhs=vw[:].bitcast(FP8X4),
+                rhs_scale=vs[:],
+                start=True,
+                stop=True,
+            )
+            st[("o", j, i)] = o_ps
 
         def m2(j):
-            gw, gs = st[("gw", j)]
-            for i in range(2):
-                o_ps = psum.tile([P, O], F32, name="o%d" % i, tag="o%d" % i, bufs=1)
-                nc.tensor.matmul_mx(
-                    out=o_ps[:],
-                    lhsT=gw[:, i * P : (i + 1) * P].bitcast(FP8X4),
-                    lhsT_scale=gs[:, i * P : (i + 1) * P],
-                    rhs=vw[:].bitcast(FP8X4),
-                    rhs_scale=vs[:],
-                    start=True,
-                    stop=True,
-                )
-                st[("o", j, i)] = o_ps
+            m2t(j, 0)
+            m2t(j, 1)
 
-        def eo_s(j):
-            o_sb = work.tile([P, 2, O], F32, name="o_sb", tag="o_sb", bufs=4)
-            nc.scalar.copy(out=o_sb[:, 0, :], in_=st[("o", j, 0)][:])
-            st[("o_sb", j)] = o_sb
+        def eo(j, i, scalar):
+            if i == 0:
+                st[("o_sb", j)] = work.tile([P, 2, O], F32, name="o_sb", tag="o_sb", bufs=4)
+            copy_on(scalar)(out=st[("o_sb", j)][:, i, :], in_=st[("o", j, i)][:])
 
-        def eo_v(j):
+        def store(j):
             qt, r0, ov = src[j]
-            o_sb = st[("o_sb", j)]
-            nc.vector.tensor_copy(out=o_sb[:, 1, :], in_=st[("o", j, 1)][:])
-            nc.sync.dma_start(out=ov[:, r0 : r0 + 2, :], in_=o_sb[:])
-
-        def prep_v():
-            vg = const.tile([P, O, 4], BF16, name="vg", align_bytes=64)
-            nc.vector.tensor_copy(out=vg[:], in_=v_sb[:].rearrange("p j o -> p o j"))
-            return vg
+            nc.sync.dma_start(out=ov[:, r0 : r0 + 2, :], in_=st[("o_sb", j)][:])
 
         def ok(j):
             return 0 <= j < NP
 
-        vg = None
-        for kk in range(-2, NP + 3):
-            if ok(kk):
-                sq(kk, 0)
+        def scalar_takes(j):
+            return j < 27 and j % 4 != 0
+
+        k_flip(0, False)
+        k_flip(1, True)
+        tq(0, "gT")
+        k_quant(0)
+        eq(0)
+        tq(1, "o0")
+        k_quant(1)
+        qq(0)
+        m1(0, 0)
+        m1(0, 1)
+        eq(1)
+        qq(1)
+
+        for kk in range(0, NP):
+            sq(kk, 0)
             if ok(kk - 2):
                 tg(kk - 2)
             if ok(kk + 2):
                 tq(kk + 2)
-            if ok(kk):
+            if kk > 0:
                 m1(kk, 1)
             if ok(kk - 3):
                 m2(kk - 3)
@@ -227,16 +277,15 @@ def tile_pinard_t_kernel(tc, q, k, v, out):
                 m1(kk + 1, 0)
             if ok(kk - 1):
                 ge(kk - 1, 1)
-            if ok(kk):
-                sq(kk, 1)
-            if ok(kk - 3):
-                eo_s(kk - 3)
+            sq(kk, 1)
+            if ok(kk - 3) and scalar_takes(kk - 3):
+                eo(kk - 3, 0, True)
             if ok(kk - 2):
                 eg(kk - 2)
             if ok(kk + 2):
                 eq(kk + 2)
             if kk == 0:
-                vg = prep_v()
+                nc.vector.tensor_copy(out=vg[:], in_=v_sb[:].rearrange("p j o -> p o j"))
             if ok(kk - 2):
                 qg_(kk - 2)
             if ok(kk + 2):
@@ -246,4 +295,35 @@ def tile_pinard_t_kernel(tc, q, k, v, out):
                     out=vw[:].bitcast(FP8X4), scales=vs[:], in_=vg[:].rearrange("p o j -> p (o j)")
                 )
             if ok(kk - 3):
-                eo_v(kk - 3)
+                if not scalar_takes(kk - 3):
+                    eo(kk - 3, 0, False)
+                eo(kk - 3, 1, False)
+                store(kk - 3)
+
+        last = NP - 1
+        tg(last - 1)
+        m2(last - 2)
+        ge(last, 0)
+        tgt(last, 0, "qT")
+        eo(last - 2, 0, True)
+        eo(last - 2, 1, True)
+        store(last - 2)
+        ge(last, 1)
+        tgt(last, 1, "sc")
+        eg(last - 1)
+        new_gg(last)
+        egt(last, 0, False)
+        qg_(last - 1)
+        m2(last - 1)
+        new_gw(last)
+        qgt(last, 0)
+        egt(last, 1, True)
+        eo(last - 1, 0, True)
+        eo(last - 1, 1, False)
+        store(last - 1)
+        m2t(last, 0)
+        qgt(last, 1)
+        m2t(last, 1)
+        eo(last, 0, True)
+        eo(last, 1, False)
+        store(last)

@@ -215,38 +215,62 @@ def tile_pinard_t_kernel(tc, q, k, v, out):
                 in_=st[("gg", j)][:, i, :, :].rearrange("p r t -> p (r t)"),
             )
 
-        def m2t(j, i):
-            gw, gs = st[("gw", j)]
-            o_ps = bank([P, O], F32, "o%d" % i)
-            nc.tensor.matmul_mx(
-                out=o_ps[:],
-                lhsT=gw[:, i * P : (i + 1) * P].bitcast(FP8X4),
-                lhsT_scale=gs[:, i * P : (i + 1) * P],
-                rhs=vw[:].bitcast(FP8X4),
-                rhs_scale=vs[:],
-                start=True,
-                stop=True,
+        def ecb(j):
+            gc = work.tile([P, 4, P], BF16, name="gc", tag="gc", bufs=2)
+            nc.vector.tensor_copy(out=gc[:], in_=st[("gT", j)][:, 1, :, :])
+            st[("gc", j)] = gc
+
+        def rg(j):
+            new_gg(j)
+            nc.gpsimd.tensor_scalar(
+                out=st[("gg", j)][:, 1, :, :],
+                in0=st[("gc", j)][:].rearrange("p t r -> p r t"),
+                scalar1=1.0,
+                scalar2=0.0,
+                op0=ALU.mult,
+                op1=ALU.add,
             )
-            st[("o", j, i)] = o_ps
+
+        def ega(j):
+            nc.vector.tensor_copy(
+                out=st[("gg", j)][:, 0, :, :],
+                in_=st[("gT", j)][:, 0, :, :].rearrange("p t r -> p r t"),
+            )
 
         def m2(j):
-            m2t(j, 0)
-            m2t(j, 1)
+            gw, gs = st[("gw", j)]
+            small = bank([P, P], F32, "o0")
+            big = bank([P, 3 * P], F32, "o1")
+            dsts = (small[:], big[:, 0:P], big[:, P : 2 * P], big[:, 2 * P : 3 * P])
+            for piece in range(4):
+                i = piece // 2
+                h = piece % 2
+                nc.tensor.matmul_mx(
+                    out=dsts[piece],
+                    lhsT=gw[:, i * P : (i + 1) * P].bitcast(FP8X4),
+                    lhsT_scale=gs[:, i * P : (i + 1) * P],
+                    rhs=vw[:, h * P : (h + 1) * P].bitcast(FP8X4),
+                    rhs_scale=vs[:, h * P : (h + 1) * P],
+                    start=True,
+                    stop=True,
+                )
+            st[("o", j)] = (small, big)
 
-        def eo(j, i, scalar):
-            if i == 0:
-                st[("o_sb", j)] = work.tile([P, 2, O], F32, name="o_sb", tag="o_sb", bufs=4)
-            copy_on(scalar)(out=st[("o_sb", j)][:, i, :], in_=st[("o", j, i)][:])
+        def eo_small(j, scalar):
+            st[("o_sb", j)] = work.tile([P, 2 * O], F32, name="o_sb", tag="o_sb", bufs=4)
+            copy_on(scalar)(out=st[("o_sb", j)][:, 0:P], in_=st[("o", j)][0][:])
+
+        def eo_big(j, scalar):
+            copy_on(scalar)(out=st[("o_sb", j)][:, P : 4 * P], in_=st[("o", j)][1][:])
 
         def store(j):
             qt, r0, ov = src[j]
-            nc.sync.dma_start(out=ov[:, r0 : r0 + 2, :], in_=st[("o_sb", j)][:])
+            nc.sync.dma_start(
+                out=ov[:, r0 : r0 + 2, :], in_=st[("o_sb", j)][:].rearrange("p (i o) -> p i o", i=2)
+            )
 
         def ok(j):
             return 0 <= j < NP
-
-        def scalar_takes(j):
-            return j < 27 and j % 4 != 0
 
         k_flip(0, False)
         k_flip(1, True)
@@ -265,48 +289,48 @@ def tile_pinard_t_kernel(tc, q, k, v, out):
             sq(kk, 0)
             if ok(kk - 2):
                 tg(kk - 2)
+                ecb(kk - 2)
+                rg(kk - 2)
             if ok(kk + 2):
                 tq(kk + 2)
-            if kk > 0:
-                m1(kk, 1)
             if ok(kk - 3):
                 m2(kk - 3)
             if ok(kk - 1):
                 ge(kk - 1, 0)
             if ok(kk + 1):
                 m1(kk + 1, 0)
+            sq(kk, 1)
             if ok(kk - 1):
                 ge(kk - 1, 1)
-            sq(kk, 1)
-            if ok(kk - 3) and scalar_takes(kk - 3):
-                eo(kk - 3, 0, True)
+            if ok(kk + 1):
+                m1(kk + 1, 1)
+            if ok(kk - 3):
+                eo_small(kk - 3, True)
             if ok(kk - 2):
-                eg(kk - 2)
+                ega(kk - 2)
             if ok(kk + 2):
                 eq(kk + 2)
             if kk == 0:
                 nc.vector.tensor_copy(out=vg[:], in_=v_sb[:].rearrange("p j o -> p o j"))
-            if ok(kk - 2):
-                qg_(kk - 2)
+            if ok(kk - 3):
+                eo_big(kk - 3, False)
+                store(kk - 3)
             if ok(kk + 2):
                 qq(kk + 2)
             if kk == 0:
                 nc.vector.quantize_mx(
                     out=vw[:].bitcast(FP8X4), scales=vs[:], in_=vg[:].rearrange("p o j -> p (o j)")
                 )
-            if ok(kk - 3):
-                if not scalar_takes(kk - 3):
-                    eo(kk - 3, 0, False)
-                eo(kk - 3, 1, False)
-                store(kk - 3)
+            if ok(kk - 2):
+                qg_(kk - 2)
 
         last = NP - 1
         tg(last - 1)
         m2(last - 2)
         ge(last, 0)
         tgt(last, 0, "qT")
-        eo(last - 2, 0, True)
-        eo(last - 2, 1, True)
+        eo_small(last - 2, True)
+        eo_big(last - 2, True)
         store(last - 2)
         ge(last, 1)
         tgt(last, 1, "sc")
@@ -318,12 +342,11 @@ def tile_pinard_t_kernel(tc, q, k, v, out):
         new_gw(last)
         qgt(last, 0)
         egt(last, 1, True)
-        eo(last - 1, 0, True)
-        eo(last - 1, 1, False)
+        eo_small(last - 1, True)
+        eo_big(last - 1, False)
         store(last - 1)
-        m2t(last, 0)
         qgt(last, 1)
-        m2t(last, 1)
-        eo(last, 0, True)
-        eo(last, 1, False)
+        m2(last)
+        eo_small(last, True)
+        eo_big(last, False)
         store(last)

@@ -18,7 +18,7 @@ D = 512
 NB = 512
 O = 256
 FLOPS = 2 * TOKENS * D * NB + 2 * TOKENS * NB * O
-CHUNKS = (2, 2, 4, 8, 8, 8, 8, 8, 8, 8)
+CHUNKS = (2, 4, 8, 8, 8, 8, 8, 8, 8)
 NP = TOKENS // (2 * P)
 
 
@@ -34,14 +34,17 @@ def tile_pinard_t_kernel(tc, q, k, v, out):
         ctx.enter_context(tc.manual_schedule())
 
         kv = k.rearrange("(p t) d -> p t d", t=4)
-        k_sb = []
-        for h in range(2):
-            kt = const.tile([P, 2, D], BF16, name="k_sb%d" % h)
-            nc.sync.dma_start(out=kt[:], in_=kv[:, 2 * h : 2 * h + 2, :])
-            k_sb.append(kt)
+        k_sb = [const.tile([P, D], BF16, name="k_sb%d" % t) for t in range(4)]
+        q_first = [const.tile([P, D], BF16, name="q_first%d" % i) for i in range(2)]
         v_sb = const.tile([P, 4, O], BF16, name="v_sb")
-        src = []
-        row = 0
+        for t in (0, 1):
+            nc.sync.dma_start(out=k_sb[t][:], in_=kv[:, t, :])
+        nc.sync.dma_start(out=q_first[0][:], in_=qf[0:P, :])
+        for t in (2, 3):
+            nc.sync.dma_start(out=k_sb[t][:], in_=kv[:, t, :])
+        nc.sync.dma_start(out=q_first[1][:], in_=qf[P : 2 * P, :])
+        src = [(q_first[0][:], q_first[1][:], of[0 : 2 * P, :].rearrange("(i p) o -> p i o", i=2))]
+        row = 2 * P
         for c, rows in enumerate(CHUNKS):
             qt = qpool.tile([P, rows, D], BF16, name="q%d" % c, tag="q%d" % c)
             nc.sync.dma_start(
@@ -49,9 +52,9 @@ def tile_pinard_t_kernel(tc, q, k, v, out):
             )
             ov = of[row : row + P * rows, :].rearrange("(p r) o -> p r o", r=rows)
             for r0 in range(0, rows, 2):
-                src.append((qt, r0, ov))
+                src.append((qt[:, r0, :], qt[:, r0 + 1, :], ov[:, r0 : r0 + 2, :]))
             row += P * rows
-            if c == 2:
+            if c == 1:
                 nc.sync.dma_start(out=v_sb[:], in_=v.rearrange("(p j) o -> p j o", j=4))
 
         warm = const.tile([P, 1], F32, name="warm")
@@ -79,11 +82,16 @@ def tile_pinard_t_kernel(tc, q, k, v, out):
         def copy_on(scalar):
             return nc.scalar.copy if scalar else nc.vector.tensor_copy
 
-        def flip_pair(dst, rows):
-            for i in range(2):
-                words = rows[i].bitcast(F32)
-                for u in range(2):
-                    nc.tensor.transpose(dst[:, i, u, :], words[:, u * P : (u + 1) * P], ident_f[:])
+        def flip_tile(dst, rows):
+            words = rows.bitcast(F32)
+            for u in range(2):
+                nc.tensor.transpose(dst[:, u, :], words[:, u * P : (u + 1) * P], ident_f[:])
+
+        def regroup_tile(scalar, dst, ps):
+            copy_on(scalar)(
+                out=dst.bitcast(F32).rearrange("p (t u) -> p t u", u=2),
+                in_=ps[:].rearrange("p u t -> p t u"),
+            )
 
         def regroup_words(scalar, dst, ps):
             copy_on(scalar)(
@@ -91,24 +99,43 @@ def tile_pinard_t_kernel(tc, q, k, v, out):
                 in_=ps[:].rearrange("p i u t -> p i t u"),
             )
 
-        def k_flip(h, scalar):
-            ps = bank([P, 2, 2, P], F32, "sc")
-            flip_pair(ps, [k_sb[h][:, 0, :], k_sb[h][:, 1, :]])
-            kg = const.tile([P, 8 * P], BF16, name="kg%d" % h, align_bytes=64)
-            regroup_words(scalar, kg, ps)
-            st[("kg", h)] = kg
+        kg = const.tile([P, 4 * D], BF16, name="kg", align_bytes=64)
 
-        def k_quant(h):
+        def k_flip(t, scalar):
+            ps = bank([P, 2, P], F32, "sc")
+            flip_tile(ps, k_sb[t][:])
+            regroup_tile(scalar, kg[:, t * D : (t + 1) * D], ps)
+
+        def k_quant(t):
             nc.vector.quantize_mx(
-                out=kw[:, 256 * h : 256 * h + 256].bitcast(FP8X4),
-                scales=ks[:, 256 * h : 256 * h + 256],
-                in_=st[("kg", h)][:],
+                out=kw[:, t * P : (t + 1) * P].bitcast(FP8X4),
+                scales=ks[:, t * P : (t + 1) * P],
+                in_=kg[:, t * D : (t + 1) * D],
+            )
+
+        def first_flip(i, tag, scalar):
+            if i == 0:
+                st[("qg", 0)] = work.tile([P, 8 * P], BF16, name="qg", tag="qg", bufs=2, align_bytes=64)
+            ps = bank([P, 2, P], F32, tag)
+            flip_tile(ps, src[0][i])
+            regroup_tile(scalar, st[("qg", 0)][:, i * D : (i + 1) * D], ps)
+
+        def first_quant(i):
+            if i == 0:
+                qw = work.tile([P, 2 * P], U32, name="qw", tag="qw", bufs=4, align_bytes=64)
+                qs = work.tile([P, 2 * P], U8, name="qs", tag="qs", bufs=4, align_bytes=64)
+                st[("qw", 0)] = (qw, qs)
+            qw, qs = st[("qw", 0)]
+            nc.vector.quantize_mx(
+                out=qw[:, i * P : (i + 1) * P].bitcast(FP8X4),
+                scales=qs[:, i * P : (i + 1) * P],
+                in_=st[("qg", 0)][:, i * D : (i + 1) * D],
             )
 
         def tq(j, tag="qT"):
-            qt, r0, ov = src[j]
             ps = bank([P, 2, 2, P], F32, tag)
-            flip_pair(ps, [qt[:, r0, :], qt[:, r0 + 1, :]])
+            for i in range(2):
+                flip_tile(ps[:, i, :, :], src[j][i])
             st[("qT", j)] = ps
 
         def eq(j):
@@ -215,72 +242,52 @@ def tile_pinard_t_kernel(tc, q, k, v, out):
                 in_=st[("gg", j)][:, i, :, :].rearrange("p r t -> p (r t)"),
             )
 
-        def ecb(j):
-            gc = work.tile([P, 4, P], BF16, name="gc", tag="gc", bufs=2)
-            nc.vector.tensor_copy(out=gc[:], in_=st[("gT", j)][:, 1, :, :])
-            st[("gc", j)] = gc
-
-        def rg(j):
-            new_gg(j)
-            nc.gpsimd.tensor_scalar(
-                out=st[("gg", j)][:, 1, :, :],
-                in0=st[("gc", j)][:].rearrange("p t r -> p r t"),
-                scalar1=1.0,
-                scalar2=0.0,
-                op0=ALU.mult,
-                op1=ALU.add,
+        def m2t(j, i):
+            gw, gs = st[("gw", j)]
+            o_ps = bank([P, O], F32, "o%d" % i)
+            nc.tensor.matmul_mx(
+                out=o_ps[:],
+                lhsT=gw[:, i * P : (i + 1) * P].bitcast(FP8X4),
+                lhsT_scale=gs[:, i * P : (i + 1) * P],
+                rhs=vw[:].bitcast(FP8X4),
+                rhs_scale=vs[:],
+                start=True,
+                stop=True,
             )
-
-        def ega(j):
-            nc.vector.tensor_copy(
-                out=st[("gg", j)][:, 0, :, :],
-                in_=st[("gT", j)][:, 0, :, :].rearrange("p t r -> p r t"),
-            )
+            st[("o", j, i)] = o_ps
 
         def m2(j):
-            gw, gs = st[("gw", j)]
-            small = bank([P, P], F32, "o0")
-            big = bank([P, 3 * P], F32, "o1")
-            dsts = (small[:], big[:, 0:P], big[:, P : 2 * P], big[:, 2 * P : 3 * P])
-            for piece in range(4):
-                i = piece // 2
-                h = piece % 2
-                nc.tensor.matmul_mx(
-                    out=dsts[piece],
-                    lhsT=gw[:, i * P : (i + 1) * P].bitcast(FP8X4),
-                    lhsT_scale=gs[:, i * P : (i + 1) * P],
-                    rhs=vw[:, h * P : (h + 1) * P].bitcast(FP8X4),
-                    rhs_scale=vs[:, h * P : (h + 1) * P],
-                    start=True,
-                    stop=True,
-                )
-            st[("o", j)] = (small, big)
+            m2t(j, 0)
+            m2t(j, 1)
 
-        def eo_small(j, scalar):
-            st[("o_sb", j)] = work.tile([P, 2 * O], F32, name="o_sb", tag="o_sb", bufs=4)
-            copy_on(scalar)(out=st[("o_sb", j)][:, 0:P], in_=st[("o", j)][0][:])
-
-        def eo_big(j, scalar):
-            copy_on(scalar)(out=st[("o_sb", j)][:, P : 4 * P], in_=st[("o", j)][1][:])
+        def eo(j, i, scalar):
+            if i == 0:
+                st[("o_sb", j)] = work.tile([P, 2, O], F32, name="o_sb", tag="o_sb", bufs=4)
+            copy_on(scalar)(out=st[("o_sb", j)][:, i, :], in_=st[("o", j, i)][:])
 
         def store(j):
-            qt, r0, ov = src[j]
-            nc.sync.dma_start(
-                out=ov[:, r0 : r0 + 2, :], in_=st[("o_sb", j)][:].rearrange("p (i o) -> p i o", i=2)
-            )
+            nc.sync.dma_start(out=src[j][2], in_=st[("o_sb", j)][:])
 
         def ok(j):
             return 0 <= j < NP
 
+        def scalar_takes(j):
+            return j < 27
+
         k_flip(0, False)
         k_flip(1, True)
-        tq(0, "gT")
         k_quant(0)
-        eq(0)
-        tq(1, "o0")
+        first_flip(0, "gT", False)
+        k_flip(2, True)
         k_quant(1)
-        qq(0)
+        first_quant(0)
+        k_flip(3, False)
+        first_flip(1, "o0", True)
+        k_quant(2)
+        k_quant(3)
+        tq(1, "o1")
         m1(0, 0)
+        first_quant(1)
         m1(0, 1)
         eq(1)
         qq(1)
@@ -289,48 +296,48 @@ def tile_pinard_t_kernel(tc, q, k, v, out):
             sq(kk, 0)
             if ok(kk - 2):
                 tg(kk - 2)
-                ecb(kk - 2)
-                rg(kk - 2)
             if ok(kk + 2):
                 tq(kk + 2)
+            if kk > 0:
+                m1(kk, 1)
             if ok(kk - 3):
                 m2(kk - 3)
             if ok(kk - 1):
                 ge(kk - 1, 0)
             if ok(kk + 1):
                 m1(kk + 1, 0)
-            sq(kk, 1)
             if ok(kk - 1):
                 ge(kk - 1, 1)
-            if ok(kk + 1):
-                m1(kk + 1, 1)
-            if ok(kk - 3):
-                eo_small(kk - 3, True)
+            sq(kk, 1)
+            if ok(kk - 3) and scalar_takes(kk - 3):
+                eo(kk - 3, 0, True)
             if ok(kk - 2):
-                ega(kk - 2)
+                eg(kk - 2)
             if ok(kk + 2):
                 eq(kk + 2)
             if kk == 0:
                 nc.vector.tensor_copy(out=vg[:], in_=v_sb[:].rearrange("p j o -> p o j"))
-            if ok(kk - 3):
-                eo_big(kk - 3, False)
-                store(kk - 3)
+            if ok(kk - 2):
+                qg_(kk - 2)
             if ok(kk + 2):
                 qq(kk + 2)
             if kk == 0:
                 nc.vector.quantize_mx(
                     out=vw[:].bitcast(FP8X4), scales=vs[:], in_=vg[:].rearrange("p o j -> p (o j)")
                 )
-            if ok(kk - 2):
-                qg_(kk - 2)
+            if ok(kk - 3):
+                if not scalar_takes(kk - 3):
+                    eo(kk - 3, 0, False)
+                eo(kk - 3, 1, False)
+                store(kk - 3)
 
         last = NP - 1
         tg(last - 1)
         m2(last - 2)
         ge(last, 0)
         tgt(last, 0, "qT")
-        eo_small(last - 2, True)
-        eo_big(last - 2, True)
+        eo(last - 2, 0, True)
+        eo(last - 2, 1, True)
         store(last - 2)
         ge(last, 1)
         tgt(last, 1, "sc")
@@ -342,11 +349,12 @@ def tile_pinard_t_kernel(tc, q, k, v, out):
         new_gw(last)
         qgt(last, 0)
         egt(last, 1, True)
-        eo_small(last - 1, True)
-        eo_big(last - 1, False)
+        eo(last - 1, 0, True)
+        eo(last - 1, 1, False)
         store(last - 1)
+        m2t(last, 0)
         qgt(last, 1)
-        m2(last)
-        eo_small(last, True)
-        eo_big(last, False)
+        m2t(last, 1)
+        eo(last, 0, True)
+        eo(last, 1, False)
         store(last)

@@ -65,8 +65,6 @@ def tile_pinard_t_kernel(tc, q, k, v, out):
         nc.scalar.activation(out=warm2[:], in_=warm[:], func=ACT.Gelu)
         ident_f = const.tile([P, P], F32, name="ident_f")
         make_identity(nc, ident_f[:])
-        ident_b = const.tile([P, P], BF16, name="ident_b")
-        make_identity(nc, ident_b[:])
         junk = const.tile([P, NB], BF16, name="junk")
         kw = const.tile([P, NB], U32, name="kw", align_bytes=64)
         ks = const.tile([P, NB], U8, name="ks", align_bytes=64)
@@ -184,41 +182,35 @@ def tile_pinard_t_kernel(tc, q, k, v, out):
             if i == 0:
                 st[("g", j)] = work.tile([P, 2, NB], BF16, name="g", tag="g", bufs=2)
             nc.scalar.activation(
-                out=st[("g", j)][:, i, :],
-                in_=st[("sc", j, i)][:],
+                out=st[("g", j)][:, i, :].rearrange("p (u r e) -> p u r e", u=2, e=2),
+                in_=st[("sc", j, i)][:].rearrange("p (u e r) -> p u r e", u=2, e=2),
                 func=ACT.Gelu,
                 scale=st[("rn", j)][:, i : i + 1],
             )
 
         def tg_tile(j, i, dst):
-            g = st[("g", j)]
-            for t in range(4):
-                nc.tensor.transpose(dst[:, t, :], g[:, i, t * P : (t + 1) * P], ident_b[:])
+            flip_tile(dst, st[("g", j)][:, i, :])
 
         def tg(j):
-            ps = bank([P, 2, 4, P], BF16, "gT")
+            ps = bank([P, 2, 2, P], F32, "gT")
             for i in range(2):
                 tg_tile(j, i, ps[:, i, :, :])
             st[("gT", j)] = ps
 
         def tgt(j, i, tag):
-            ps = bank([P, 4, P], BF16, tag)
+            ps = bank([P, 2, P], F32, tag)
             tg_tile(j, i, ps)
             st[("gT", j, i)] = ps
 
         def new_gg(j):
-            st[("gg", j)] = work.tile([P, 2, P, 4], BF16, name="gg", tag="gg", bufs=2, align_bytes=64)
+            st[("gg", j)] = work.tile([P, 8 * P], BF16, name="gg", tag="gg", bufs=2, align_bytes=64)
 
         def eg(j):
             new_gg(j)
-            nc.vector.tensor_copy(
-                out=st[("gg", j)][:], in_=st[("gT", j)][:].rearrange("p i t r -> p i r t")
-            )
+            regroup_words(False, st[("gg", j)], st[("gT", j)])
 
         def egt(j, i, scalar):
-            copy_on(scalar)(
-                out=st[("gg", j)][:, i, :, :], in_=st[("gT", j, i)][:].rearrange("p t r -> p r t")
-            )
+            regroup_tile(scalar, st[("gg", j)][:, i * NB : (i + 1) * NB], st[("gT", j, i)])
 
         def new_gw(j):
             gw = work.tile([P, 2 * P], U32, name="gw", tag="gw", bufs=4, align_bytes=64)
@@ -231,7 +223,7 @@ def tile_pinard_t_kernel(tc, q, k, v, out):
             nc.vector.quantize_mx(
                 out=gw[:].bitcast(FP8X4),
                 scales=gs[:],
-                in_=st[("gg", j)][:].rearrange("p i r t -> p (i r t)"),
+                in_=st[("gg", j)][:],
             )
 
         def qgt(j, i):
@@ -239,7 +231,7 @@ def tile_pinard_t_kernel(tc, q, k, v, out):
             nc.vector.quantize_mx(
                 out=gw[:, i * P : (i + 1) * P].bitcast(FP8X4),
                 scales=gs[:, i * P : (i + 1) * P],
-                in_=st[("gg", j)][:, i, :, :].rearrange("p r t -> p (r t)"),
+                in_=st[("gg", j)][:, i * NB : (i + 1) * NB],
             )
 
         def m2t(j, i):

@@ -71,7 +71,7 @@ def tile_pinard_t_kernel(tc, q, k, v, out):
         vw = const.tile([P, O], U32, name="vw", align_bytes=64)
         vs = const.tile([P, O], U8, name="vs", align_bytes=64)
         vg = const.tile([P, O, 4], BF16, name="vg", align_bytes=64)
-        bank_bufs = {"sc": 4, "qT": 1, "gT": 1, "o0": 1, "o1": 1}
+        bank_bufs = {"sc": 4, "qT": 1, "gT": 1, "o": 2}
         st = {}
 
         def bank(shape, dtype, tag):
@@ -234,11 +234,10 @@ def tile_pinard_t_kernel(tc, q, k, v, out):
                 in_=st[("gg", j)][:, i * NB : (i + 1) * NB],
             )
 
-        def m2t(j, i):
+        def m2t(j, i, dst):
             gw, gs = st[("gw", j)]
-            o_ps = bank([P, O], F32, "o%d" % i)
             nc.tensor.matmul_mx(
-                out=o_ps[:],
+                out=dst,
                 lhsT=gw[:, i * P : (i + 1) * P].bitcast(FP8X4),
                 lhsT_scale=gs[:, i * P : (i + 1) * P],
                 rhs=vw[:].bitcast(FP8X4),
@@ -246,25 +245,28 @@ def tile_pinard_t_kernel(tc, q, k, v, out):
                 start=True,
                 stop=True,
             )
-            st[("o", j, i)] = o_ps
 
         def m2(j):
-            m2t(j, 0)
-            m2t(j, 1)
+            ps = bank([P, 2, O], F32, "o")
+            for i in range(2):
+                m2t(j, i, ps[:, i, :])
+            st[("o", j)] = ps
 
-        def eo(j, i, scalar):
-            if i == 0:
-                st[("o_sb", j)] = work.tile([P, 2, O], F32, name="o_sb", tag="o_sb", bufs=4)
-            copy_on(scalar)(out=st[("o_sb", j)][:, i, :], in_=st[("o", j, i)][:])
+        def new_o_sb(j):
+            st[("o_sb", j)] = work.tile([P, 2, O], F32, name="o_sb", tag="o_sb", bufs=4)
+
+        def eo(j, scalar):
+            new_o_sb(j)
+            copy_on(scalar)(out=st[("o_sb", j)][:], in_=st[("o", j)][:])
+
+        def eot(j, i, scalar, ps):
+            copy_on(scalar)(out=st[("o_sb", j)][:, i, :], in_=ps[:])
 
         def store(j):
             nc.sync.dma_start(out=src[j][2], in_=st[("o_sb", j)][:])
 
         def ok(j):
             return 0 <= j < NP
-
-        def scalar_takes(j):
-            return j < 27
 
         k_flip(0, False)
         k_flip(1, True)
@@ -274,10 +276,10 @@ def tile_pinard_t_kernel(tc, q, k, v, out):
         k_quant(1)
         first_quant(0)
         k_flip(3, False)
-        first_flip(1, "o0", True)
+        first_flip(1, "o", True)
         k_quant(2)
         k_quant(3)
-        tq(1, "o1")
+        tq(1, "o")
         m1(0, 0)
         first_quant(1)
         m1(0, 1)
@@ -301,8 +303,6 @@ def tile_pinard_t_kernel(tc, q, k, v, out):
             if ok(kk - 1):
                 ge(kk - 1, 1)
             sq(kk, 1)
-            if ok(kk - 3) and scalar_takes(kk - 3):
-                eo(kk - 3, 0, True)
             if ok(kk - 2):
                 eg(kk - 2)
             if ok(kk + 2):
@@ -318,9 +318,7 @@ def tile_pinard_t_kernel(tc, q, k, v, out):
                     out=vw[:].bitcast(FP8X4), scales=vs[:], in_=vg[:].rearrange("p o j -> p (o j)")
                 )
             if ok(kk - 3):
-                if not scalar_takes(kk - 3):
-                    eo(kk - 3, 0, False)
-                eo(kk - 3, 1, False)
+                eo(kk - 3, False)
                 store(kk - 3)
 
         last = NP - 1
@@ -328,8 +326,7 @@ def tile_pinard_t_kernel(tc, q, k, v, out):
         m2(last - 2)
         ge(last, 0)
         tgt(last, 0, "qT")
-        eo(last - 2, 0, True)
-        eo(last - 2, 1, True)
+        eo(last - 2, True)
         store(last - 2)
         ge(last, 1)
         tgt(last, 1, "sc")
@@ -341,12 +338,13 @@ def tile_pinard_t_kernel(tc, q, k, v, out):
         new_gw(last)
         qgt(last, 0)
         egt(last, 1, True)
-        eo(last - 1, 0, True)
-        eo(last - 1, 1, False)
+        eo(last - 1, True)
         store(last - 1)
-        m2t(last, 0)
+        o_last = [bank([P, O], F32, "gT"), bank([P, O], F32, "o")]
+        new_o_sb(last)
+        m2t(last, 0, o_last[0][:])
         qgt(last, 1)
-        m2t(last, 1)
-        eo(last, 0, True)
-        eo(last, 1, False)
+        m2t(last, 1, o_last[1][:])
+        eot(last, 0, True, o_last[0])
+        eot(last, 1, False, o_last[1])
         store(last)

@@ -93,7 +93,7 @@ def tile_pinard_t_kernel(tc, q, k, v, out):
 
         def regroup_words(scalar, dst, ps):
             copy_on(scalar)(
-                out=dst[:].bitcast(F32).rearrange("p (i t u) -> p i t u", i=2, u=2),
+                out=dst.bitcast(F32).rearrange("p (i t u) -> p i t u", i=2, u=2),
                 in_=ps[:].rearrange("p i u t -> p i t u"),
             )
 
@@ -138,7 +138,7 @@ def tile_pinard_t_kernel(tc, q, k, v, out):
 
         def eq(j):
             qg = work.tile([P, 8 * P], BF16, name="qg", tag="qg", bufs=2, align_bytes=64)
-            regroup_words(False, qg, st[("qT", j)])
+            regroup_words(False, qg[:], st[("qT", j)])
             st[("qg", j)] = qg
 
         def qq(j):
@@ -207,7 +207,7 @@ def tile_pinard_t_kernel(tc, q, k, v, out):
 
         def eg(j):
             new_gg(j)
-            regroup_words(False, st[("gg", j)], st[("gT", j)])
+            regroup_words(False, st[("gg", j)][:], st[("gT", j)])
 
         def egt(j, i, scalar):
             regroup_tile(scalar, st[("gg", j)][:, i * NB : (i + 1) * NB], st[("gT", j, i)])
@@ -268,6 +268,19 @@ def tile_pinard_t_kernel(tc, q, k, v, out):
         def ok(j):
             return 0 <= j < NP
 
+        def regroup_both(kk):
+            x = work.tile([P, 16 * P], BF16, name="x", tag="x", bufs=2, align_bytes=64)
+            regroup_words(False, x[:, 0 : 8 * P], st[("gT", kk - 2)])
+            regroup_words(False, x[:, 8 * P : 16 * P], st[("qT", kk + 2)])
+            st[("x", kk)] = x
+
+        def quant_both(kk):
+            xw = work.tile([P, 4 * P], U32, name="xw", tag="xw", bufs=4, align_bytes=64)
+            xs = work.tile([P, 4 * P], U8, name="xs", tag="xs", bufs=4, align_bytes=64)
+            nc.vector.quantize_mx(out=xw[:].bitcast(FP8X4), scales=xs[:], in_=st[("x", kk)][:])
+            st[("gw", kk - 2)] = (xw[:, 0 : 2 * P], xs[:, 0 : 2 * P])
+            st[("qw", kk + 2)] = (xw[:, 2 * P : 4 * P], xs[:, 2 * P : 4 * P])
+
         k_flip(0, False)
         k_flip(1, True)
         k_quant(0)
@@ -303,23 +316,28 @@ def tile_pinard_t_kernel(tc, q, k, v, out):
             if ok(kk - 1):
                 ge(kk - 1, 1)
             sq(kk, 1)
-            if ok(kk - 2):
+            both = ok(kk - 2) and ok(kk + 2)
+            if both:
+                regroup_both(kk)
+            elif ok(kk - 2):
                 eg(kk - 2)
-            if ok(kk + 2):
+            elif ok(kk + 2):
                 eq(kk + 2)
             if kk == 0:
                 nc.vector.tensor_copy(out=vg[:], in_=v_sb[:].rearrange("p j o -> p o j"))
-            if ok(kk - 2):
+            if ok(kk - 3):
+                eo(kk - 3, False)
+                store(kk - 3)
+            if both:
+                quant_both(kk)
+            elif ok(kk - 2):
                 qg_(kk - 2)
-            if ok(kk + 2):
+            elif ok(kk + 2):
                 qq(kk + 2)
             if kk == 0:
                 nc.vector.quantize_mx(
                     out=vw[:].bitcast(FP8X4), scales=vs[:], in_=vg[:].rearrange("p o j -> p (o j)")
                 )
-            if ok(kk - 3):
-                eo(kk - 3, False)
-                store(kk - 3)
 
         last = NP - 1
         tg(last - 1)

@@ -71,7 +71,7 @@ def tile_pinard_t_kernel(tc, q, k, v, out):
         vw = const.tile([P, O], U32, name="vw", align_bytes=64)
         vs = const.tile([P, O], U8, name="vs", align_bytes=64)
         vg = const.tile([P, O, 4], BF16, name="vg", align_bytes=64)
-        bank_bufs = {"sc": 4, "qT": 1, "gT": 1, "o": 2}
+        bank_bufs = {"sc": 5, "qT": 1, "gT": 1, "o": 1}
         st = {}
 
         def bank(shape, dtype, tag):
@@ -289,7 +289,7 @@ def tile_pinard_t_kernel(tc, q, k, v, out):
         k_quant(1)
         first_quant(0)
         k_flip(3, False)
-        first_flip(1, "o", True)
+        first_flip(1, "sc", True)
         k_quant(2)
         k_quant(3)
         tq(1, "o")
@@ -301,21 +301,20 @@ def tile_pinard_t_kernel(tc, q, k, v, out):
 
         for kk in range(0, NP):
             sq(kk, 0)
+            sq(kk, 1)
             if ok(kk - 2):
                 tg(kk - 2)
             if ok(kk + 2):
                 tq(kk + 2)
-            if kk > 0:
-                m1(kk, 1)
+            if ok(kk + 1):
+                m1(kk + 1, 0)
             if ok(kk - 3):
                 m2(kk - 3)
             if ok(kk - 1):
                 ge(kk - 1, 0)
-            if ok(kk + 1):
-                m1(kk + 1, 0)
-            if ok(kk - 1):
                 ge(kk - 1, 1)
-            sq(kk, 1)
+            if ok(kk + 1):
+                m1(kk + 1, 1)
             both = ok(kk - 2) and ok(kk + 2)
             if both:
                 regroup_both(kk)
@@ -344,10 +343,10 @@ def tile_pinard_t_kernel(tc, q, k, v, out):
         m2(last - 2)
         ge(last, 0)
         tgt(last, 0, "qT")
-        eo(last - 2, True)
-        store(last - 2)
         ge(last, 1)
         tgt(last, 1, "sc")
+        eo(last - 2, True)
+        store(last - 2)
         eg(last - 1)
         new_gg(last)
         egt(last, 0, False)
@@ -358,7 +357,7 @@ def tile_pinard_t_kernel(tc, q, k, v, out):
         egt(last, 1, True)
         eo(last - 1, True)
         store(last - 1)
-        o_last = [bank([P, O], F32, "gT"), bank([P, O], F32, "o")]
+        o_last = [bank([P, O], F32, "gT"), bank([P, O], F32, "sc")]
         new_o_sb(last)
         m2t(last, 0, o_last[0][:])
         qgt(last, 1)

@@ -136,9 +136,9 @@ def tile_pinard_t_kernel(tc, q, k, v, out):
                 flip_tile(ps[:, i, :, :], src[j][i])
             st[("qT", j)] = ps
 
-        def eq(j):
+        def eq(j, scalar=False):
             qg = work.tile([P, 8 * P], BF16, name="qg", tag="qg", bufs=2, align_bytes=64)
-            regroup_words(False, qg[:], st[("qT", j)])
+            regroup_words(scalar, qg[:], st[("qT", j)])
             st[("qg", j)] = qg
 
         def qq(j):
@@ -191,11 +191,18 @@ def tile_pinard_t_kernel(tc, q, k, v, out):
         def tg_tile(j, i, dst):
             flip_tile(dst, st[("g", j)][:, i, :])
 
+        def new_gT(j):
+            st[("gT", j)] = bank([P, 2, 2, P], F32, "gT")
+
+        def warm_pe(j):
+            nc.tensor.matmul(
+                st[("gT", j)][:, 0, 0, :], lhsT=ident_f[:], rhs=ident_f[:], start=True, stop=True
+            )
+
         def tg(j):
-            ps = bank([P, 2, 2, P], F32, "gT")
+            ps = st[("gT", j)]
             for i in range(2):
                 tg_tile(j, i, ps[:, i, :, :])
-            st[("gT", j)] = ps
 
         def tgt(j, i, tag):
             ps = bank([P, 2, P], F32, tag)
@@ -271,15 +278,15 @@ def tile_pinard_t_kernel(tc, q, k, v, out):
         def regroup_both(kk):
             x = work.tile([P, 16 * P], BF16, name="x", tag="x", bufs=2, align_bytes=64)
             regroup_words(False, x[:, 0 : 8 * P], st[("gT", kk - 2)])
-            regroup_words(False, x[:, 8 * P : 16 * P], st[("qT", kk + 2)])
+            regroup_words(False, x[:, 8 * P : 16 * P], st[("qT", kk + 3)])
             st[("x", kk)] = x
 
         def quant_both(kk):
-            xw = work.tile([P, 4 * P], U32, name="xw", tag="xw", bufs=4, align_bytes=64)
-            xs = work.tile([P, 4 * P], U8, name="xs", tag="xs", bufs=4, align_bytes=64)
+            xw = work.tile([P, 4 * P], U32, name="xw", tag="xw", bufs=6, align_bytes=64)
+            xs = work.tile([P, 4 * P], U8, name="xs", tag="xs", bufs=6, align_bytes=64)
             nc.vector.quantize_mx(out=xw[:].bitcast(FP8X4), scales=xs[:], in_=st[("x", kk)][:])
             st[("gw", kk - 2)] = (xw[:, 0 : 2 * P], xs[:, 0 : 2 * P])
-            st[("qw", kk + 2)] = (xw[:, 2 * P : 4 * P], xs[:, 2 * P : 4 * P])
+            st[("qw", kk + 3)] = (xw[:, 2 * P : 4 * P], xs[:, 2 * P : 4 * P])
 
         k_flip(0, False)
         k_flip(1, True)
@@ -296,44 +303,54 @@ def tile_pinard_t_kernel(tc, q, k, v, out):
         m1(0, 0)
         first_quant(1)
         m1(0, 1)
-        eq(1)
+        tq(2)
+        eq(1, True)
         qq(1)
 
         for kk in range(0, NP):
+            both = ok(kk - 2) and ok(kk + 3)
             sq(kk, 0)
             sq(kk, 1)
-            if ok(kk - 2):
-                tg(kk - 2)
-            if ok(kk + 2):
-                tq(kk + 2)
             if ok(kk + 1):
                 m1(kk + 1, 0)
+            if kk == 0:
+                m1(1, 1)
+                eq(2)
+                tq(3, "gT")
+                eq(3)
+                qq(2)
+                qq(3)
+            if ok(kk - 2):
+                tg(kk - 2)
+            if both:
+                tq(kk + 3)
+                regroup_both(kk)
+            elif ok(kk - 2):
+                eg(kk - 2)
+            elif kk == 1:
+                tq(4)
+                eq(4)
             if ok(kk - 3):
                 m2(kk - 3)
             if ok(kk - 1):
                 ge(kk - 1, 0)
                 ge(kk - 1, 1)
-            if ok(kk + 1):
+            if kk > 0 and ok(kk + 1):
                 m1(kk + 1, 1)
-            both = ok(kk - 2) and ok(kk + 2)
-            if both:
-                regroup_both(kk)
-            elif ok(kk - 2):
-                eg(kk - 2)
-            elif ok(kk + 2):
-                eq(kk + 2)
-            if kk == 0:
-                nc.vector.tensor_copy(out=vg[:], in_=v_sb[:].rearrange("p j o -> p o j"))
+            if ok(kk - 1):
+                new_gT(kk - 1)
+                warm_pe(kk - 1)
             if ok(kk - 3):
                 eo(kk - 3, False)
                 store(kk - 3)
+            if kk == 1:
+                nc.vector.tensor_copy(out=vg[:], in_=v_sb[:].rearrange("p j o -> p o j"))
+                qq(4)
             if both:
                 quant_both(kk)
             elif ok(kk - 2):
                 qg_(kk - 2)
-            elif ok(kk + 2):
-                qq(kk + 2)
-            if kk == 0:
+            if kk == 1:
                 nc.vector.quantize_mx(
                     out=vw[:].bitcast(FP8X4), scales=vs[:], in_=vg[:].rearrange("p o j -> p (o j)")
                 )

@@ -65,7 +65,7 @@ def tile_pinard_t_kernel(tc, q, k, v, out):
         nc.scalar.activation(out=warm2[:], in_=warm[:], func=ACT.Gelu)
         ident_f = const.tile([P, P], F32, name="ident_f")
         make_identity(nc, ident_f[:])
-        junk = const.tile([P, NB], BF16, name="junk")
+        junk = [const.tile([P, NB], BF16, name="junk%d" % i) for i in range(2)]
         kw = const.tile([P, NB], U32, name="kw", align_bytes=64)
         ks = const.tile([P, NB], U8, name="ks", align_bytes=64)
         vw = const.tile([P, O], U32, name="vw", align_bytes=64)
@@ -168,7 +168,7 @@ def tile_pinard_t_kernel(tc, q, k, v, out):
             ms = st[("ms", j)]
             rn = st[("rn", j)]
             nc.scalar.activation(
-                out=junk[:],
+                out=junk[i][:],
                 in_=st[("sc", j, i)][:],
                 func=ACT.Square,
                 scale=1.0 / math.sqrt(float(NB)),

@@ -59,13 +59,13 @@ def tile_pinard_t_kernel(tc, q, k, v, out):
 
         warm = const.tile([P, 1], F32, name="warm")
         warm2 = const.tile([P, 1], F32, name="warm2")
-        neghalf = const.tile([P, 1], F32, name="neghalf")
+        neghalf = const.tile([P, 2], F32, name="neghalf")
         nc.vector.memset(warm[:], 0.0)
         nc.vector.memset(neghalf[:], -0.5)
         nc.scalar.activation(out=warm2[:], in_=warm[:], func=ACT.Gelu)
         ident_f = const.tile([P, P], F32, name="ident_f")
         make_identity(nc, ident_f[:])
-        junk = [const.tile([P, NB], BF16, name="junk%d" % i) for i in range(2)]
+        junk = [const.tile([P, NB], BF16, name="junk%d" % i) for i in range(4)]
         kw = const.tile([P, NB], U32, name="kw", align_bytes=64)
         ks = const.tile([P, NB], U8, name="ks", align_bytes=64)
         vw = const.tile([P, O], U32, name="vw", align_bytes=64)
@@ -147,6 +147,21 @@ def tile_pinard_t_kernel(tc, q, k, v, out):
             nc.vector.quantize_mx(out=qw[:].bitcast(FP8X4), scales=qs[:], in_=st[("qg", j)][:])
             st[("qw", j)] = (qw, qs)
 
+        def m1_by_column_tiles(j, i):
+            qw, qs = st[("qw", j)]
+            sc = bank([P, NB], F32, "sc")
+            for t in range(4):
+                nc.tensor.matmul_mx(
+                    out=sc[:, t * P : (t + 1) * P],
+                    lhsT=qw[:, i * P : (i + 1) * P].bitcast(FP8X4),
+                    lhsT_scale=qs[:, i * P : (i + 1) * P],
+                    rhs=kw[:, t * P : (t + 1) * P].bitcast(FP8X4),
+                    rhs_scale=ks[:, t * P : (t + 1) * P],
+                    start=True,
+                    stop=True,
+                )
+            st[("sc", j, i)] = sc
+
         def m1(j, i):
             qw, qs = st[("qw", j)]
             sc = bank([P, NB], F32, "sc")
@@ -168,15 +183,14 @@ def tile_pinard_t_kernel(tc, q, k, v, out):
             ms = st[("ms", j)]
             rn = st[("rn", j)]
             nc.scalar.activation(
-                out=junk[i][:],
+                out=junk[2 * (j % 2) + i][:],
                 in_=st[("sc", j, i)][:],
                 func=ACT.Square,
                 scale=1.0 / math.sqrt(float(NB)),
                 accum_out=ms[:, i : i + 1],
             )
-            nc.gpsimd.tensor_tensor(
-                out=rn[:, i : i + 1], in0=ms[:, i : i + 1], in1=neghalf[:], op=ALU.pow
-            )
+            if i == 1:
+                nc.gpsimd.tensor_tensor(out=rn[:], in0=ms[:], in1=neghalf[:], op=ALU.pow)
 
         def ge(j, i):
             if i == 0:
@@ -253,14 +267,14 @@ def tile_pinard_t_kernel(tc, q, k, v, out):
                 stop=True,
             )
 
-        def m2(j):
-            ps = bank([P, 2, O], F32, "o")
+        def m2(j, tag="o"):
+            ps = bank([P, 2, O], F32, tag)
             for i in range(2):
                 m2t(j, i, ps[:, i, :])
             st[("o", j)] = ps
 
         def new_o_sb(j):
-            st[("o_sb", j)] = work.tile([P, 2, O], F32, name="o_sb", tag="o_sb", bufs=4)
+            st[("o_sb", j)] = work.tile([P, 2, O], F32, name="o_sb", tag="o_sb", bufs=NP)
 
         def eo(j, scalar):
             new_o_sb(j)
@@ -276,7 +290,7 @@ def tile_pinard_t_kernel(tc, q, k, v, out):
             return 0 <= j < NP
 
         def regroup_both(kk):
-            x = work.tile([P, 16 * P], BF16, name="x", tag="x", bufs=2, align_bytes=64)
+            x = work.tile([P, 16 * P], BF16, name="x", tag="x", bufs=4, align_bytes=64)
             regroup_words(False, x[:, 0 : 8 * P], st[("gT", kk - 2)])
             regroup_words(False, x[:, 8 * P : 16 * P], st[("qT", kk + 3)])
             st[("x", kk)] = x
@@ -288,6 +302,9 @@ def tile_pinard_t_kernel(tc, q, k, v, out):
             st[("gw", kk - 2)] = (xw[:, 0 : 2 * P], xs[:, 0 : 2 * P])
             st[("qw", kk + 3)] = (xw[:, 2 * P : 4 * P], xs[:, 2 * P : 4 * P])
 
+        wake = bank([P, P], F32, "o")
+        for n in range(3):
+            nc.tensor.matmul(wake[:], lhsT=ident_f[:], rhs=ident_f[:], start=True, stop=True)
         k_flip(0, False)
         k_flip(1, True)
         k_quant(0)
@@ -295,19 +312,19 @@ def tile_pinard_t_kernel(tc, q, k, v, out):
         k_flip(2, True)
         k_quant(1)
         first_quant(0)
-        k_flip(3, False)
+        k_flip(3, True)
         first_flip(1, "sc", True)
         k_quant(2)
         k_quant(3)
         tq(1, "o")
-        m1(0, 0)
+        m1_by_column_tiles(0, 0)
         first_quant(1)
-        m1(0, 1)
+        m1_by_column_tiles(0, 1)
         tq(2)
         eq(1, True)
         qq(1)
 
-        for kk in range(0, NP):
+        for kk in range(0, NP - 1):
             both = ok(kk - 2) and ok(kk + 3)
             sq(kk, 0)
             sq(kk, 1)
@@ -356,29 +373,45 @@ def tile_pinard_t_kernel(tc, q, k, v, out):
                 )
 
         last = NP - 1
-        tg(last - 1)
-        m2(last - 2)
+        prev = last - 1
+        sq(last, 0)
+        sq(last, 1)
+        tg(prev - 1)
+        m2(prev - 2)
+        eg(prev - 1)
+        new_gT(prev)
+        warm_pe(prev)
+        eo(prev - 2, False)
+        store(prev - 2)
+        qg_(prev - 1)
+        ge(prev, 0)
+        tgt(prev, 0, "qT")
+        m2(prev - 1)
+        ge(prev, 1)
+        tgt(prev, 1, "sc")
+        new_gg(prev)
+        egt(prev, 0, False)
         ge(last, 0)
-        tgt(last, 0, "qT")
-        ge(last, 1)
-        tgt(last, 1, "sc")
-        eo(last - 2, True)
-        store(last - 2)
-        eg(last - 1)
+        tgt(last, 0, "gT")
+        egt(prev, 1, False)
         new_gg(last)
         egt(last, 0, False)
-        qg_(last - 1)
-        m2(last - 1)
+        qg_(prev)
+        ge(last, 1)
+        tgt(last, 1, "sc")
+        m2(prev, "sc")
+        eo(prev - 1, True)
+        store(prev - 1)
+        egt(last, 1, True)
         new_gw(last)
         qgt(last, 0)
-        egt(last, 1, True)
-        eo(last - 1, True)
-        store(last - 1)
-        o_last = [bank([P, O], F32, "gT"), bank([P, O], F32, "sc")]
+        o_last = [bank([P, O], F32, "qT"), bank([P, O], F32, "gT")]
         new_o_sb(last)
         m2t(last, 0, o_last[0][:])
         qgt(last, 1)
         m2t(last, 1, o_last[1][:])
-        eot(last, 0, True, o_last[0])
+        eo(prev, True)
+        store(prev)
+        eot(last, 0, False, o_last[0])
         eot(last, 1, False, o_last[1])
         store(last)

from contextlib import ExitStack
import math

import concourse.mybir as mybir
from concourse.masks import make_identity

F32 = mybir.dt.float32
BF16 = mybir.dt.bfloat16
U32 = mybir.dt.uint32
U8 = mybir.dt.uint8
FP8X4 = mybir.dt.float8_e4m3fn_x4
ACT = mybir.ActivationFunctionType
ALU = mybir.AluOpType

P = 128
TOKENS = 8192
D = 512
NB = 512
O = 256
FLOPS = 2 * TOKENS * D * NB + 2 * TOKENS * NB * O
CHUNKS = (2, 4, 8, 8, 8, 8, 8, 8, 8)
NP = TOKENS // (2 * P)


def tile_pinard_t_kernel(tc, q, k, v, out):
    nc = tc.nc
    qf = q.flatten_outer_dims()
    of = out.flatten_outer_dims()
    with ExitStack() as ctx:
        const = ctx.enter_context(tc.tile_pool(name="const", bufs=1))
        qpool = ctx.enter_context(tc.tile_pool(name="qpool", bufs=1))
        work = ctx.enter_context(tc.tile_pool(name="work", bufs=2))
        psum = ctx.enter_context(tc.psum_pool(name="psum", bufs=1))
        ctx.enter_context(tc.manual_schedule())

        kv = k.rearrange("(p t) d -> p t d", t=4)
        k_sb = [const.tile([P, D], BF16, name="k_sb%d" % t) for t in range(4)]
        q_first = [const.tile([P, D], BF16, name="q_first%d" % i) for i in range(2)]
        v_sb = const.tile([P, 4, O], BF16, name="v_sb")
        for t in (0, 1):
            nc.sync.dma_start(out=k_sb[t][:], in_=kv[:, t, :])
        nc.sync.dma_start(out=q_first[0][:], in_=qf[0:P, :])
        for t in (2, 3):
            nc.sync.dma_start(out=k_sb[t][:], in_=kv[:, t, :])
        nc.sync.dma_start(out=q_first[1][:], in_=qf[P : 2 * P, :])
        src = [(q_first[0][:], q_first[1][:], of[0 : 2 * P, :].rearrange("(i p) o -> p i o", i=2))]
        row = 2 * P
        for c, rows in enumerate(CHUNKS):
            qt = qpool.tile([P, rows, D], BF16, name="q%d" % c, tag="q%d" % c)
            nc.sync.dma_start(
                out=qt[:], in_=qf[row : row + P * rows, :].rearrange("(p r) d -> p r d", r=rows)
            )
            ov = of[row : row + P * rows, :].rearrange("(p r) o -> p r o", r=rows)
            for r0 in range(0, rows, 2):
                src.append((qt[:, r0, :], qt[:, r0 + 1, :], ov[:, r0 : r0 + 2, :]))
            row += P * rows
            if c == 1:
                nc.sync.dma_start(out=v_sb[:], in_=v.rearrange("(p j) o -> p j o", j=4))

        warm = const.tile([P, 1], F32, name="warm")
        warm2 = const.tile([P, 1], F32, name="warm2")
        neghalf = const.tile([P, 2], F32, name="neghalf")
        nc.vector.memset(warm[:], 0.0)
        nc.vector.memset(neghalf[:], -0.5)
        nc.scalar.activation(out=warm2[:], in_=warm[:], func=ACT.Gelu)
        ident_f = const.tile([P, P], F32, name="ident_f")
        make_identity(nc, ident_f[:])
        junk = [const.tile([P, NB], BF16, name="junk%d" % i) for i in range(4)]
        kw = const.tile([P, NB], U32, name="kw", align_bytes=64)
        ks = const.tile([P, NB], U8, name="ks", align_bytes=64)
        vw = const.tile([P, O], U32, name="vw", align_bytes=64)
        vs = const.tile([P, O], U8, name="vs", align_bytes=64)
        vg = const.tile([P, O, 4], BF16, name="vg", align_bytes=64)
        bank_bufs = {"sc": 5, "qT": 1, "gT": 1, "o": 1}
        st = {}

        def bank(shape, dtype, tag):
            return psum.tile(shape, dtype, name=tag, tag=tag, bufs=bank_bufs[tag])

        def copy_on(scalar):
            return nc.scalar.copy if scalar else nc.vector.tensor_copy

        def flip_tile(dst, rows):
            words = rows.bitcast(F32)
            for u in range(2):
                nc.tensor.transpose(dst[:, u, :], words[:, u * P : (u + 1) * P], ident_f[:])

        def regroup_tile(scalar, dst, ps):
            copy_on(scalar)(
                out=dst.bitcast(F32).rearrange("p (t u) -> p t u", u=2),
                in_=ps[:].rearrange("p u t -> p t u"),
            )

        def regroup_words(scalar, dst, ps):
            copy_on(scalar)(
                out=dst.bitcast(F32).rearrange("p (i t u) -> p i t u", i=2, u=2),
                in_=ps[:].rearrange("p i u t -> p i t u"),
            )

        kg = const.tile([P, 4 * D], BF16, name="kg", align_bytes=64)

        def k_flip(t, scalar):
            ps = bank([P, 2, P], F32, "sc")
            flip_tile(ps, k_sb[t][:])
            regroup_tile(scalar, kg[:, t * D : (t + 1) * D], ps)

        def k_quant(t):
            nc.vector.quantize_mx(
                out=kw[:, t * P : (t + 1) * P].bitcast(FP8X4),
                scales=ks[:, t * P : (t + 1) * P],
                in_=kg[:, t * D : (t + 1) * D],
            )

        def first_flip(i, tag, scalar):
            if i == 0:
                st[("qg", 0)] = work.tile([P, 8 * P], BF16, name="qg", tag="qg", bufs=2, align_bytes=64)
            ps = bank([P, 2, P], F32, tag)
            flip_tile(ps, src[0][i])
            regroup_tile(scalar, st[("qg", 0)][:, i * D : (i + 1) * D], ps)

        def first_quant(i):
            if i == 0:
                qw = work.tile([P, 2 * P], U32, name="qw", tag="qw", bufs=4, align_bytes=64)
                qs = work.tile([P, 2 * P], U8, name="qs", tag="qs", bufs=4, align_bytes=64)
                st[("qw", 0)] = (qw, qs)
            qw, qs = st[("qw", 0)]
            nc.vector.quantize_mx(
                out=qw[:, i * P : (i + 1) * P].bitcast(FP8X4),
                scales=qs[:, i * P : (i + 1) * P],
                in_=st[("qg", 0)][:, i * D : (i + 1) * D],
            )

        def tq(j, tag="qT"):
            ps = bank([P, 2, 2, P], F32, tag)
            for i in range(2):
                flip_tile(ps[:, i, :, :], src[j][i])
            st[("qT", j)] = ps

        def eq(j, scalar=False):
            qg = work.tile([P, 8 * P], BF16, name="qg", tag="qg", bufs=2, align_bytes=64)
            regroup_words(scalar, qg[:], st[("qT", j)])
            st[("qg", j)] = qg

        def qq(j):
            qw = work.tile([P, 2 * P], U32, name="qw", tag="qw", bufs=4, align_bytes=64)
            qs = work.tile([P, 2 * P], U8, name="qs", tag="qs", bufs=4, align_bytes=64)
            nc.vector.quantize_mx(out=qw[:].bitcast(FP8X4), scales=qs[:], in_=st[("qg", j)][:])
            st[("qw", j)] = (qw, qs)

        def m1_by_column_tiles(j, i):
            qw, qs = st[("qw", j)]
            sc = bank([P, NB], F32, "sc")
            for t in range(4):
                nc.tensor.matmul_mx(
                    out=sc[:, t * P : (t + 1) * P],
                    lhsT=qw[:, i * P : (i + 1) * P].bitcast(FP8X4),
                    lhsT_scale=qs[:, i * P : (i + 1) * P],
                    rhs=kw[:, t * P : (t + 1) * P].bitcast(FP8X4),
                    rhs_scale=ks[:, t * P : (t + 1) * P],
                    start=True,
                    stop=True,
                )
            st[("sc", j, i)] = sc

        def m1(j, i):
            qw, qs = st[("qw", j)]
            sc = bank([P, NB], F32, "sc")
            nc.tensor.matmul_mx(
                out=sc[:],
                lhsT=qw[:, i * P : (i + 1) * P].bitcast(FP8X4),
                lhsT_scale=qs[:, i * P : (i + 1) * P],
                rhs=kw[:].bitcast(FP8X4),
                rhs_scale=ks[:],
                start=True,
                stop=True,
            )
            st[("sc", j, i)] = sc

        def sq(j, i):
            if i == 0:
                st[("ms", j)] = work.tile([P, 2], F32, name="ms", tag="ms", bufs=4)
                st[("rn", j)] = work.tile([P, 2], F32, name="rn", tag="rn", bufs=4)
            ms = st[("ms", j)]
            rn = st[("rn", j)]
            nc.scalar.activation(
                out=junk[2 * (j % 2) + i][:],
                in_=st[("sc", j, i)][:],
                func=ACT.Square,
                scale=1.0 / math.sqrt(float(NB)),
                accum_out=ms[:, i : i + 1],
            )
            if i == 1:
                nc.gpsimd.tensor_tensor(out=rn[:], in0=ms[:], in1=neghalf[:], op=ALU.pow)

        def ge(j, i):
            if i == 0:
                st[("g", j)] = work.tile([P, 2, NB], BF16, name="g", tag="g", bufs=2)
            nc.scalar.activation(
                out=st[("g", j)][:, i, :].rearrange("p (u r e) -> p u r e", u=2, e=2),
                in_=st[("sc", j, i)][:].rearrange("p (u e r) -> p u r e", u=2, e=2),
                func=ACT.Gelu,
                scale=st[("rn", j)][:, i : i + 1],
            )

        def tg_tile(j, i, dst):
            flip_tile(dst, st[("g", j)][:, i, :])

        def new_gT(j):
            st[("gT", j)] = bank([P, 2, 2, P], F32, "gT")

        def warm_pe(j):
            nc.tensor.matmul(
                st[("gT", j)][:, 0, 0, :], lhsT=ident_f[:], rhs=ident_f[:], start=True, stop=True
            )

        def tg(j):
            ps = st[("gT", j)]
            for i in range(2):
                tg_tile(j, i, ps[:, i, :, :])

        def tgt(j, i, tag):
            ps = bank([P, 2, P], F32, tag)
            tg_tile(j, i, ps)
            st[("gT", j, i)] = ps

        def new_gg(j):
            st[("gg", j)] = work.tile([P, 8 * P], BF16, name="gg", tag="gg", bufs=2, align_bytes=64)

        def eg(j):
            new_gg(j)
            regroup_words(False, st[("gg", j)][:], st[("gT", j)])

        def egt(j, i, scalar):
            regroup_tile(scalar, st[("gg", j)][:, i * NB : (i + 1) * NB], st[("gT", j, i)])

        def new_gw(j):
            gw = work.tile([P, 2 * P], U32, name="gw", tag="gw", bufs=4, align_bytes=64)
            gs = work.tile([P, 2 * P], U8, name="gs", tag="gs", bufs=4, align_bytes=64)
            st[("gw", j)] = (gw, gs)

        def qg_(j):
            new_gw(j)
            gw, gs = st[("gw", j)]
            nc.vector.quantize_mx(
                out=gw[:].bitcast(FP8X4),
                scales=gs[:],
                in_=st[("gg", j)][:],
            )

        def qgt(j, i):
            gw, gs = st[("gw", j)]
            nc.vector.quantize_mx(
                out=gw[:, i * P : (i + 1) * P].bitcast(FP8X4),
                scales=gs[:, i * P : (i + 1) * P],
                in_=st[("gg", j)][:, i * NB : (i + 1) * NB],
            )

        def m2t(j, i, dst):
            gw, gs = st[("gw", j)]
            nc.tensor.matmul_mx(
                out=dst,
                lhsT=gw[:, i * P : (i + 1) * P].bitcast(FP8X4),
                lhsT_scale=gs[:, i * P : (i + 1) * P],
                rhs=vw[:].bitcast(FP8X4),
                rhs_scale=vs[:],
                start=True,
                stop=True,
            )

        def m2(j, tag="o"):
            ps = bank([P, 2, O], F32, tag)
            for i in range(2):
                m2t(j, i, ps[:, i, :])
            st[("o", j)] = ps

        def new_o_sb(j):
            st[("o_sb", j)] = work.tile([P, 2, O], F32, name="o_sb", tag="o_sb", bufs=NP)

        def eo(j, scalar):
            new_o_sb(j)
            copy_on(scalar)(out=st[("o_sb", j)][:], in_=st[("o", j)][:])

        def eot(j, i, scalar, ps):
            copy_on(scalar)(out=st[("o_sb", j)][:, i, :], in_=ps[:])

        def store(j):
            nc.sync.dma_start(out=src[j][2], in_=st[("o_sb", j)][:])

        def ok(j):
            return 0 <= j < NP

        def regroup_both(kk):
            x = work.tile([P, 16 * P], BF16, name="x", tag="x", bufs=4, align_bytes=64)
            regroup_words(False, x[:, 0 : 8 * P], st[("gT", kk - 2)])
            regroup_words(False, x[:, 8 * P : 16 * P], st[("qT", kk + 3)])
            st[("x", kk)] = x

        def quant_both(kk):
            xw = work.tile([P, 4 * P], U32, name="xw", tag="xw", bufs=6, align_bytes=64)
            xs = work.tile([P, 4 * P], U8, name="xs", tag="xs", bufs=6, align_bytes=64)
            nc.vector.quantize_mx(out=xw[:].bitcast(FP8X4), scales=xs[:], in_=st[("x", kk)][:])
            st[("gw", kk - 2)] = (xw[:, 0 : 2 * P], xs[:, 0 : 2 * P])
            st[("qw", kk + 3)] = (xw[:, 2 * P : 4 * P], xs[:, 2 * P : 4 * P])

        wake = bank([P, P], F32, "o")
        for n in range(3):
            nc.tensor.matmul(wake[:], lhsT=ident_f[:], rhs=ident_f[:], start=True, stop=True)
        k_flip(0, False)
        k_flip(1, True)
        k_quant(0)
        first_flip(0, "gT", False)
        k_flip(2, True)
        k_quant(1)
        first_quant(0)
        k_flip(3, True)
        first_flip(1, "sc", True)
        k_quant(2)
        k_quant(3)
        tq(1, "o")
        m1_by_column_tiles(0, 0)
        first_quant(1)
        m1_by_column_tiles(0, 1)
        tq(2)
        eq(1, True)
        qq(1)

        for kk in range(0, NP - 1):
            both = ok(kk - 2) and ok(kk + 3)
            sq(kk, 0)
            sq(kk, 1)
            if ok(kk + 1):
                m1(kk + 1, 0)
            if kk == 0:
                m1(1, 1)
                eq(2)
                tq(3, "gT")
                eq(3)
                qq(2)
                qq(3)
            if ok(kk - 2):
                tg(kk - 2)
            if both:
                tq(kk + 3)
                regroup_both(kk)
            elif ok(kk - 2):
                eg(kk - 2)
            elif kk == 1:
                tq(4)
                eq(4)
            if ok(kk - 3):
                m2(kk - 3)
            if ok(kk - 1):
                ge(kk - 1, 0)
                ge(kk - 1, 1)
            if kk > 0 and ok(kk + 1):
                m1(kk + 1, 1)
            if ok(kk - 1):
                new_gT(kk - 1)
                warm_pe(kk - 1)
            if ok(kk - 3):
                eo(kk - 3, False)
                store(kk - 3)
            if kk == 1:
                nc.vector.tensor_copy(out=vg[:], in_=v_sb[:].rearrange("p j o -> p o j"))
                qq(4)
            if both:
                quant_both(kk)
            elif ok(kk - 2):
                qg_(kk - 2)
            if kk == 1:
                nc.vector.quantize_mx(
                    out=vw[:].bitcast(FP8X4), scales=vs[:], in_=vg[:].rearrange("p o j -> p (o j)")
                )

        last = NP - 1
        prev = last - 1
        sq(last, 0)
        sq(last, 1)
        tg(prev - 1)
        m2(prev - 2)
        eg(prev - 1)
        new_gT(prev)
        warm_pe(prev)
        eo(prev - 2, False)
        store(prev - 2)
        qg_(prev - 1)
        ge(prev, 0)
        tgt(prev, 0, "qT")
        m2(prev - 1)
        ge(prev, 1)
        tgt(prev, 1, "sc")
        new_gg(prev)
        egt(prev, 0, False)
        ge(last, 0)
        tgt(last, 0, "gT")
        egt(prev, 1, False)
        new_gg(last)
        egt(last, 0, False)
        qg_(prev)
        ge(last, 1)
        tgt(last, 1, "sc")
        m2(prev, "sc")
        eo(prev - 1, True)
        store(prev - 1)
        egt(last, 1, True)
        new_gw(last)
        qgt(last, 0)
        o_last = [bank([P, O], F32, "qT"), bank([P, O], F32, "gT")]
        new_o_sb(last)
        m2t(last, 0, o_last[0][:])
        qgt(last, 1)
        m2t(last, 1, o_last[1][:])
        eo(prev, True)
        store(prev)
        eot(last, 0, False, o_last[0])
        eot(last, 1, False, o_last[1])
        store(last)
